import numpy as np
import ml_dtypes


def mxq(x, axis, fmt="e4m3"):
    dtype, down = {"e4m3": (ml_dtypes.float8_e4m3fn, 7), "e5m2": (ml_dtypes.float8_e5m2, 14)}[fmt]
    v = np.moveaxis(np.asarray(x, np.float32).astype(ml_dtypes.bfloat16).astype(np.float64), axis, -1)
    blocks = v.reshape(v.shape[:-1] + (-1, 32))
    amax = np.abs(blocks).max(-1, keepdims=True)
    byte = np.maximum(np.where(amax > 0, np.frexp(amax)[1] - 1 + 127, 0) - down, 1)
    scale = np.exp2(byte - 127.0)
    codes = (blocks / scale).astype(np.float32).astype(dtype).astype(np.float64)
    return np.moveaxis((codes * scale).reshape(v.shape), -1, axis)


WIDE = False


def mx_kscale(k):
    if not WIDE:
        return np.ones(k)
    levels = np.array([10, -10, 5, -5, 0])
    a = np.random.permutation(np.resize(levels, k // 512 * 4)).reshape(k // 512, 4)
    idx = np.arange(k)
    return np.exp2(a[idx // 512, idx % 128 // 32])


BF16 = ml_dtypes.bfloat16


def bf(x):
    return np.asarray(x, np.float32).astype(BF16)


def f64(x):
    return np.asarray(x).astype(np.float64)


G, D1, D2, D3, K, N = 4, 8, 16, 16, 1024, 256

EPS = 1e-6


def setup_inputs():
    s = mx_kscale(K)
    rows = np.random.standard_normal((G, D1, D2, D3, K))
    rows = rows * (0.5 + 1.5 * np.random.random_sample((G, D1, D2, D3, 1))) + 0.5 * np.random.standard_normal((G, D1, D2, D3, 1))
    return {"x": bf(rows.reshape(G * K, D1, D2, D3)),
            "ln_gamma": bf((1.0 + 0.1 * np.random.standard_normal((G, K))) * s),
            "ln_beta": bf(0.1 * np.random.standard_normal((G, K)) * s),
            "W": bf(np.random.standard_normal((G, N, K)) / np.sqrt(K) / s),
            "b": bf(0.1 * np.random.standard_normal((G, N)))}


def reference(x, ln_gamma, ln_beta, W, b):
    xg = f64(x).reshape(G, D1, D2, D3, K)
    mu = np.mean(xg, axis=-1, keepdims=True)
    var = np.mean(np.square(xg - mu), axis=-1, keepdims=True)
    xn = (xg - mu) / np.sqrt(var + EPS)
    xn = xn * f64(ln_gamma)[:, None, None, None, :] + f64(ln_beta)[:, None, None, None, :]
    a = mxq(xn.reshape(G, D1 * D2 * D3, K), 2, "e4m3")
    y = a @ mxq(f64(W), 2, "e4m3").transpose(0, 2, 1)
    y = y.reshape(G, D1, D2, D3, N) + f64(b)[:, None, None, None, :]
    y = np.moveaxis(y, 0, -2).reshape(D1, D2, D3, G * N)
    return np.transpose(y, (3, 0, 1, 2))

@@ -1,0 +1,199 @@
+from contextlib import ExitStack
+
+import concourse.bass as bass
+import concourse.mybir as mybir
+import concourse.tile as tile
+from concourse.masks import make_identity
+
+F32 = mybir.dt.float32
+BF16 = mybir.dt.bfloat16
+U32 = mybir.dt.uint32
+U8 = mybir.dt.uint8
+FP8X4 = mybir.dt.float8_e4m3fn_x4
+ALU = mybir.AluOpType
+ACT = mybir.ActivationFunctionType
+
+P = 128
+G = 4
+K = 1024
+O = 256
+POS = 2048
+UNIT = 512
+UNITS = G * POS // UNIT
+ROWT = UNIT // P
+CHUNKS = K // P
+PASSES = K // 512
+OT = O // P
+EPS = 1e-6
+
+FLOPS = 2 * G * POS * K * O
+
+Z_ENGINE = ("g", "g", "g", "s")
+
+
+def tile_groupedlinear_t_kernel(tc, x, ln_gamma, ln_beta, W, b, out):
+    nc = tc.nc
+    xv = x.rearrange("a (h b) c d -> (a h) (b c d)", h=2)
+    ov = out.rearrange("o a b c -> o (a b c)")
+
+    with ExitStack() as ctx:
+        const = ctx.enter_context(tc.tile_pool(name="const", bufs=1))
+        xpool = ctx.enter_context(tc.tile_pool(name="xpool", bufs=4))
+        zpool = ctx.enter_context(tc.tile_pool(name="zpool", bufs=12))
+        small = ctx.enter_context(tc.tile_pool(name="small", bufs=4))
+        plpool = ctx.enter_context(tc.tile_pool(name="plpool", bufs=3))
+        gqpool = ctx.enter_context(tc.tile_pool(name="gqpool", bufs=2))
+        xcpool = ctx.enter_context(tc.tile_pool(name="xcpool", bufs=3))
+        ypool = ctx.enter_context(tc.tile_pool(name="ypool", bufs=3))
+        wstage = ctx.enter_context(tc.tile_pool(name="wstage", bufs=2))
+        pst = ctx.enter_context(tc.psum_pool(name="pst", bufs=6))
+        psy = ctx.enter_context(tc.psum_pool(name="psy", bufs=2))
+
+        x_tiles = {}
+
+        def load_x(u):
+            xt = xpool.tile([P, ROWT, K], BF16, tag="x", name="xt%d" % u)
+            rows = xv[u * UNIT:(u + 1) * UNIT, :].rearrange("(j p) k -> p j k", p=P)
+            if u == 0:
+                for j in range(ROWT):
+                    nc.sync.dma_start(out=xt[:, j, :], in_=rows[:, j, :])
+            else:
+                nc.sync.dma_start(out=xt[:], in_=rows)
+            x_tiles[u] = xt
+
+        load_x(0)
+
+        prm = const.tile([P, P], BF16, name="prm")
+        nc.vector.memset(prm[:], 0.0)
+        nc.sync.dma_start(out=prm[0:32, :], in_=ln_gamma.rearrange("g (c p) -> (g c) p", p=P))
+        nc.sync.dma_start(out=prm[32:64, :], in_=ln_beta.rearrange("g (c p) -> (g c) p", p=P))
+        nc.sync.dma_start(out=prm[64:72, :], in_=b.rearrange("g (c p) -> (g c) p", p=P))
+
+        w_raw = []
+        for g in range(G):
+            wr = const.tile([P, OT, K], BF16, name="wraw%d" % g)
+            w_raw.append(wr)
+
+        def load_w(g):
+            nc.sync.dma_start(out=w_raw[g][:], in_=W[g].rearrange("(t o) k -> o t k", t=OT))
+
+        load_w(0)
+        load_x(1)
+
+        ident_f = const.tile([P, P], F32, name="ident_f")
+        make_identity(nc, ident_f[:])
+        ident_b = const.tile([P, P], BF16, name="ident_b")
+        make_identity(nc, ident_b[:])
+        eps_t = const.tile([P, 1], F32, name="eps_t")
+        nc.vector.memset(eps_t[:], EPS)
+
+        prm_ps = pst.tile([P, P], BF16, tag="zt", name="prm_ps")
+        nc.tensor.transpose(prm_ps[:], prm[:], ident_b[:])
+        cols = const.tile([P, P], F32, name="cols")
+        nc.vector.tensor_copy(out=cols[:], in_=prm_ps[:])
+
+        wc = const.tile([P, G, PASSES, O], U32, name="wc", align_bytes=64)
+        ws = const.tile([P, G, PASSES, O], U8, name="ws", align_bytes=64)
+
+        def prep_w(g):
+            for c2 in range(PASSES):
+                wt = pst.tile([P, OT, 4, P], BF16, tag="zt", name="wt%d_%d" % (g, c2))
+                for a in range(OT):
+                    for t in range(4):
+                        c = c2 * 4 + t
+                        nc.tensor.transpose(wt[:, a, t, :], w_raw[g][:, a, c * P:(c + 1) * P], ident_b[:])
+                wg = wstage.tile([P, OT, P, 4], BF16, tag="wg", name="wg%d_%d" % (g, c2), align_bytes=64)
+                nc.scalar.copy(out=wg[:], in_=wt[:].rearrange("p a t o -> p a o t"))
+                nc.vector.quantize_mx(
+                    out=wc[:, g, c2, :].bitcast(FP8X4),
+                    scales=ws[:, g, c2, :],
+                    in_=wg[:].rearrange("p a o t -> p (a o t)"),
+                )
+
+        prep_w(0)
+
+        for u in range(UNITS):
+            g = u // (POS // UNIT)
+            q = u % (POS // UNIT)
+            if u + 2 < UNITS:
+                load_x(u + 2)
+            if q == 0 and g + 1 < G:
+                load_w(g + 1)
+            xt = x_tiles[u]
+
+            st = small.tile([P, ROWT, 2, 6], F32, tag="st", name="st%d" % u)
+            mv = small.tile([P, ROWT, 2], F32, tag="mv", name="mv%d" % u)
+            for j in range(ROWT):
+                for h in range(2):
+                    nc.vector.bn_stats(out=st[:, j, h, :], in_=xt[:, j, h * 512:(h + 1) * 512])
+                nc.vector.bn_aggr(out=mv[:, j, :], in_=st[:, j, :, :].rearrange("p h s -> p (h s)"))
+            std = small.tile([P, ROWT], F32, tag="std", name="std%d" % u)
+            nc.scalar.activation(out=std[:], in_=mv[:, :, 1], func=ACT.Sqrt, bias=eps_t[:], scale=1.0)
+            rstd = small.tile([P, ROWT], F32, tag="rstd", name="rstd%d" % u)
+            nc.vector.reciprocal(out=rstd[:], in_=std[:])
+            negmu = small.tile([P, ROWT], F32, tag="negmu", name="negmu%d" % u)
+            nc.vector.tensor_scalar(out=negmu[:], in0=mv[:, :, 0], scalar1=-1.0, scalar2=None, op0=ALU.mult)
+            nmr = small.tile([P, ROWT], F32, tag="nmr", name="nmr%d" % u)
+            nc.vector.tensor_tensor(out=nmr[:], in0=negmu[:], in1=rstd[:], op=ALU.mult)
+
+            zs = []
+            for j in range(ROWT):
+                z = zpool.tile([P, K], F32, tag="z", name="z%d_%d" % (u, j))
+                eng = Z_ENGINE[j]
+                if eng == "g":
+                    nc.gpsimd.tensor_scalar(out=z[:], in0=xt[:, j, :], scalar1=negmu[:, j:j + 1],
+                                            scalar2=rstd[:, j:j + 1], op0=ALU.add, op1=ALU.mult)
+                elif eng == "v":
+                    nc.vector.tensor_scalar(out=z[:], in0=xt[:, j, :], scalar1=negmu[:, j:j + 1],
+                                            scalar2=rstd[:, j:j + 1], op0=ALU.add, op1=ALU.mult)
+                else:
+                    nc.scalar.activation(out=z[:], in_=xt[:, j, :], func=ACT.Identity,
+                                         scale=rstd[:, j:j + 1], bias=nmr[:, j:j + 1])
+                zs.append(z)
+
+            pl = plpool.tile([P, CHUNKS, UNIT], BF16, tag="pl", name="pl%d" % u)
+            for c in range(CHUNKS):
+                zp = pst.tile([P, UNIT], F32, tag="zt", name="zp%d_%d" % (u, c))
+                for j in range(ROWT):
+                    nc.tensor.transpose(zp[:, j * P:(j + 1) * P], zs[j][:, c * P:(c + 1) * P], ident_f[:])
+                gi = g * CHUNKS + c
+                nc.scalar.activation(out=pl[:, c, :], in_=zp[:], func=ACT.Identity,
+                                     scale=cols[:, gi:gi + 1], bias=cols[:, 32 + gi:33 + gi])
+
+            gq = gqpool.tile([P, PASSES, UNIT, 4], BF16, tag="gq", name="gq%d" % u, align_bytes=64)
+            xc = xcpool.tile([P, PASSES, UNIT], U32, tag="xc", name="xc%d" % u, align_bytes=64)
+            xsc = xcpool.tile([P, PASSES, UNIT], U8, tag="xsc", name="xsc%d" % u, align_bytes=64)
+            for c2 in range(PASSES):
+                nc.vector.tensor_copy(
+                    out=gq[:, c2, :, :].rearrange("p (c i) t -> p c t i", i=4),
+                    in_=pl[:, c2 * 4:(c2 + 1) * 4, :].rearrange("p t (c i) -> p c t i", i=4),
+                )
+            for c2 in range(PASSES):
+                nc.vector.quantize_mx(
+                    out=xc[:, c2, :].bitcast(FP8X4),
+                    scales=xsc[:, c2, :],
+                    in_=gq[:, c2, :, :].rearrange("p n t -> p (n t)"),
+                )
+
+            ysb = ypool.tile([P, OT, UNIT], F32, tag="y", name="y%d" % u)
+            for a in range(OT):
+                yp = psy.tile([P, UNIT], F32, tag="yp", name="yp%d_%d" % (u, a))
+                for c2 in range(PASSES):
+                    nc.tensor.matmul_mx(
+                        out=yp[:],
+                        lhsT=wc[:, g, c2, a * P:(a + 1) * P].bitcast(FP8X4),
+                        lhsT_scale=ws[:, g, c2, a * P:(a + 1) * P],
+                        rhs=xc[:, c2, :].bitcast(FP8X4),
+                        rhs_scale=xsc[:, c2, :],
+                        start=(c2 == 0),
+                        stop=(c2 == PASSES - 1),
+                    )
+                bi = 64 + g * OT + a
+                nc.scalar.activation(out=ysb[:, a, :], in_=yp[:], func=ACT.Identity,
+                                     bias=cols[:, bi:bi + 1], scale=1.0)
+            nc.sync.dma_start(
+                out=ov[g * O:(g + 1) * O, q * UNIT:(q + 1) * UNIT].rearrange("(t o) n -> o t n", t=OT),
+                in_=ysb[:],
+            )
+            if q == 2 and g + 1 < G:
+                prep_w(g + 1)

@@ -1,8 +1,6 @@
 from contextlib import ExitStack
 
-import concourse.bass as bass
 import concourse.mybir as mybir
-import concourse.tile as tile
 from concourse.masks import make_identity
 
 F32 = mybir.dt.float32
@@ -19,16 +17,19 @@ K = 1024
 O = 256
 POS = 2048
 UNIT = 512
-UNITS = G * POS // UNIT
+UPG = POS // UNIT
+UNITS = G * UPG
 ROWT = UNIT // P
 CHUNKS = K // P
 PASSES = K // 512
 OT = O // P
 EPS = 1e-6
+XBUFS = 5
 
 FLOPS = 2 * G * POS * K * O
 
 Z_ENGINE = ("g", "g", "g", "s")
+S_Z_AFTER_BANK = 5
 
 
 def tile_groupedlinear_t_kernel(tc, x, ln_gamma, ln_beta, W, b, out):
@@ -38,7 +39,7 @@ def tile_groupedlinear_t_kernel(tc, x, ln_gamma, ln_beta, W, b, out):
 
     with ExitStack() as ctx:
         const = ctx.enter_context(tc.tile_pool(name="const", bufs=1))
-        xpool = ctx.enter_context(tc.tile_pool(name="xpool", bufs=4))
+        xpool = ctx.enter_context(tc.tile_pool(name="xpool", bufs=XBUFS))
         zpool = ctx.enter_context(tc.tile_pool(name="zpool", bufs=12))
         small = ctx.enter_context(tc.tile_pool(name="small", bufs=4))
         plpool = ctx.enter_context(tc.tile_pool(name="plpool", bufs=3))
@@ -48,8 +49,22 @@ def tile_groupedlinear_t_kernel(tc, x, ln_gamma, ln_beta, W, b, out):
         wstage = ctx.enter_context(tc.tile_pool(name="wstage", bufs=2))
         pst = ctx.enter_context(tc.psum_pool(name="pst", bufs=6))
         psy = ctx.enter_context(tc.psum_pool(name="psy", bufs=2))
+        ctx.enter_context(tc.manual_schedule())
 
-        x_tiles = {}
+        x_t = {}
+        mv_t = {}
+        std_t = {}
+        rstd_t = {}
+        negmu_t = {}
+        nmr_t = {}
+        z_t = {}
+        pl_t = {}
+        xc_t = {}
+        xsc_t = {}
+        wg_t = {}
+
+        def live(u):
+            return 0 <= u < UNITS
 
         def load_x(u):
             xt = xpool.tile([P, ROWT, K], BF16, tag="x", name="xt%d" % u)
@@ -59,15 +74,7 @@ def tile_groupedlinear_t_kernel(tc, x, ln_gamma, ln_beta, W, b, out):
                     nc.sync.dma_start(out=xt[:, j, :], in_=rows[:, j, :])
             else:
                 nc.sync.dma_start(out=xt[:], in_=rows)
-            x_tiles[u] = xt
-
-        load_x(0)
-
-        prm = const.tile([P, P], BF16, name="prm")
-        nc.vector.memset(prm[:], 0.0)
-        nc.sync.dma_start(out=prm[0:32, :], in_=ln_gamma.rearrange("g (c p) -> (g c) p", p=P))
-        nc.sync.dma_start(out=prm[32:64, :], in_=ln_beta.rearrange("g (c p) -> (g c) p", p=P))
-        nc.sync.dma_start(out=prm[64:72, :], in_=b.rearrange("g (c p) -> (g c) p", p=P))
+            x_t[u] = xt
 
         w_raw = []
         for g in range(G):
@@ -77,89 +84,108 @@ def tile_groupedlinear_t_kernel(tc, x, ln_gamma, ln_beta, W, b, out):
         def load_w(g):
             nc.sync.dma_start(out=w_raw[g][:], in_=W[g].rearrange("(t o) k -> o t k", t=OT))
 
-        load_w(0)
-        load_x(1)
-
-        ident_f = const.tile([P, P], F32, name="ident_f")
-        make_identity(nc, ident_f[:])
-        ident_b = const.tile([P, P], BF16, name="ident_b")
-        make_identity(nc, ident_b[:])
+        load_x(0)
+        prm = const.tile([P, P], BF16, name="prm")
+        nc.vector.memset(prm[:], 0.0)
         eps_t = const.tile([P, 1], F32, name="eps_t")
         nc.vector.memset(eps_t[:], EPS)
+        nc.sync.dma_start(out=prm[0:32, :], in_=ln_gamma.rearrange("g (c p) -> (g c) p", p=P))
+        nc.sync.dma_start(out=prm[32:64, :], in_=ln_beta.rearrange("g (c p) -> (g c) p", p=P))
+        nc.sync.dma_start(out=prm[64:72, :], in_=b.rearrange("g (c p) -> (g c) p", p=P))
+        load_w(0)
+        for u in range(1, XBUFS - 2):
+            load_x(u)
+
+        warm = const.tile([P, 1], F32, name="warm")
+        nc.scalar.activation(out=warm[:], in_=eps_t[:], func=ACT.Sqrt)
+
+        ident_b = const.tile([P, P], BF16, name="ident_b")
+        make_identity(nc, ident_b[:])
+        ident_f = const.tile([P, P], F32, name="ident_f")
+        make_identity(nc, ident_f[:])
 
         prm_ps = pst.tile([P, P], BF16, tag="zt", name="prm_ps")
         nc.tensor.transpose(prm_ps[:], prm[:], ident_b[:])
         cols = const.tile([P, P], F32, name="cols")
-        nc.vector.tensor_copy(out=cols[:], in_=prm_ps[:])
+        nc.scalar.copy(out=cols[:], in_=prm_ps[:])
 
         wc = const.tile([P, G, PASSES, O], U32, name="wc", align_bytes=64)
         ws = const.tile([P, G, PASSES, O], U8, name="ws", align_bytes=64)
 
-        def prep_w(g):
-            for c2 in range(PASSES):
-                wt = pst.tile([P, OT, 4, P], BF16, tag="zt", name="wt%d_%d" % (g, c2))
-                for a in range(OT):
-                    for t in range(4):
-                        c = c2 * 4 + t
-                        nc.tensor.transpose(wt[:, a, t, :], w_raw[g][:, a, c * P:(c + 1) * P], ident_b[:])
-                wg = wstage.tile([P, OT, P, 4], BF16, tag="wg", name="wg%d_%d" % (g, c2), align_bytes=64)
-                nc.scalar.copy(out=wg[:], in_=wt[:].rearrange("p a t o -> p a o t"))
-                nc.vector.quantize_mx(
-                    out=wc[:, g, c2, :].bitcast(FP8X4),
-                    scales=ws[:, g, c2, :],
-                    in_=wg[:].rearrange("p a o t -> p (a o t)"),
-                )
+        def w_transpose(g, c2):
+            wt = pst.tile([P, OT, 4, P], BF16, tag="zt", name="wt%d_%d" % (g, c2))
+            for a in range(OT):
+                for t in range(4):
+                    c = c2 * 4 + t
+                    nc.tensor.transpose(wt[:, a, t, :], w_raw[g][:, a, c * P:(c + 1) * P], ident_b[:])
+            wg = wstage.tile([P, OT, P, 4], BF16, tag="wg", name="wg%d_%d" % (g, c2), align_bytes=64)
+            nc.scalar.copy(out=wg[:], in_=wt[:].rearrange("p a t o -> p a o t"))
+            wg_t[(g, c2)] = wg
 
-        prep_w(0)
+        def w_quantise(g, c2):
+            nc.vector.quantize_mx(
+                out=wc[:, g, c2, :].bitcast(FP8X4),
+                scales=ws[:, g, c2, :],
+                in_=wg_t[(g, c2)][:].rearrange("p a o t -> p (a o t)"),
+            )
 
-        for u in range(UNITS):
-            g = u // (POS // UNIT)
-            q = u % (POS // UNIT)
-            if u + 2 < UNITS:
-                load_x(u + 2)
-            if q == 0 and g + 1 < G:
-                load_w(g + 1)
-            xt = x_tiles[u]
+        w_when = {}
+        for g in range(G):
+            w_when[max(UPG * g - 2, -1)] = (g, 0)
+            w_when[max(UPG * g - 1, 0)] = (g, 1)
 
+        def stats(u):
+            xt = x_t[u]
             st = small.tile([P, ROWT, 2, 6], F32, tag="st", name="st%d" % u)
             mv = small.tile([P, ROWT, 2], F32, tag="mv", name="mv%d" % u)
             for j in range(ROWT):
                 for h in range(2):
                     nc.vector.bn_stats(out=st[:, j, h, :], in_=xt[:, j, h * 512:(h + 1) * 512])
                 nc.vector.bn_aggr(out=mv[:, j, :], in_=st[:, j, :, :].rearrange("p h s -> p (h s)"))
+            mv_t[u] = mv
+
+        def sqrt_(u):
             std = small.tile([P, ROWT], F32, tag="std", name="std%d" % u)
-            nc.scalar.activation(out=std[:], in_=mv[:, :, 1], func=ACT.Sqrt, bias=eps_t[:], scale=1.0)
+            nc.scalar.activation(out=std[:], in_=mv_t[u][:, :, 1], func=ACT.Sqrt, bias=eps_t[:], scale=1.0)
+            std_t[u] = std
+
+        def scalars(u):
             rstd = small.tile([P, ROWT], F32, tag="rstd", name="rstd%d" % u)
-            nc.vector.reciprocal(out=rstd[:], in_=std[:])
+            nc.vector.reciprocal(out=rstd[:], in_=std_t[u][:])
             negmu = small.tile([P, ROWT], F32, tag="negmu", name="negmu%d" % u)
-            nc.vector.tensor_scalar(out=negmu[:], in0=mv[:, :, 0], scalar1=-1.0, scalar2=None, op0=ALU.mult)
+            nc.vector.tensor_scalar(out=negmu[:], in0=mv_t[u][:, :, 0], scalar1=-1.0, scalar2=None, op0=ALU.mult)
             nmr = small.tile([P, ROWT], F32, tag="nmr", name="nmr%d" % u)
             nc.vector.tensor_tensor(out=nmr[:], in0=negmu[:], in1=rstd[:], op=ALU.mult)
+            rstd_t[u] = rstd
+            negmu_t[u] = negmu
+            nmr_t[u] = nmr
 
-            zs = []
+        def zrow(u, j):
+            z = zpool.tile([P, K], F32, tag="z", name="z%d_%d" % (u, j))
+            eng = Z_ENGINE[j]
+            xin = x_t[u][:, j, :]
+            if eng == "g":
+                nc.gpsimd.tensor_scalar(out=z[:], in0=xin, scalar1=negmu_t[u][:, j:j + 1],
+                                        scalar2=rstd_t[u][:, j:j + 1], op0=ALU.add, op1=ALU.mult)
+            elif eng == "v":
+                nc.vector.tensor_scalar(out=z[:], in0=xin, scalar1=negmu_t[u][:, j:j + 1],
+                                        scalar2=rstd_t[u][:, j:j + 1], op0=ALU.add, op1=ALU.mult)
+            else:
+                nc.scalar.activation(out=z[:], in_=xin, func=ACT.Identity,
+                                     scale=rstd_t[u][:, j:j + 1], bias=nmr_t[u][:, j:j + 1])
+            z_t[(u, j)] = z
+
+        def bank(u, c):
+            g = u // UPG
+            zp = pst.tile([P, UNIT], F32, tag="zt", name="zp%d_%d" % (u, c))
             for j in range(ROWT):
-                z = zpool.tile([P, K], F32, tag="z", name="z%d_%d" % (u, j))
-                eng = Z_ENGINE[j]
-                if eng == "g":
-                    nc.gpsimd.tensor_scalar(out=z[:], in0=xt[:, j, :], scalar1=negmu[:, j:j + 1],
-                                            scalar2=rstd[:, j:j + 1], op0=ALU.add, op1=ALU.mult)
-                elif eng == "v":
-                    nc.vector.tensor_scalar(out=z[:], in0=xt[:, j, :], scalar1=negmu[:, j:j + 1],
-                                            scalar2=rstd[:, j:j + 1], op0=ALU.add, op1=ALU.mult)
-                else:
-                    nc.scalar.activation(out=z[:], in_=xt[:, j, :], func=ACT.Identity,
-                                         scale=rstd[:, j:j + 1], bias=nmr[:, j:j + 1])
-                zs.append(z)
+                nc.tensor.transpose(zp[:, j * P:(j + 1) * P], z_t[(u, j)][:, c * P:(c + 1) * P], ident_f[:])
+            gi = g * CHUNKS + c
+            nc.scalar.activation(out=pl_t[u][:, c, :], in_=zp[:], func=ACT.Identity,
+                                 scale=cols[:, gi:gi + 1], bias=cols[:, 32 + gi:33 + gi])
 
-            pl = plpool.tile([P, CHUNKS, UNIT], BF16, tag="pl", name="pl%d" % u)
-            for c in range(CHUNKS):
-                zp = pst.tile([P, UNIT], F32, tag="zt", name="zp%d_%d" % (u, c))
-                for j in range(ROWT):
-                    nc.tensor.transpose(zp[:, j * P:(j + 1) * P], zs[j][:, c * P:(c + 1) * P], ident_f[:])
-                gi = g * CHUNKS + c
-                nc.scalar.activation(out=pl[:, c, :], in_=zp[:], func=ACT.Identity,
-                                     scale=cols[:, gi:gi + 1], bias=cols[:, 32 + gi:33 + gi])
-
+        def regroup_quantise(u):
+            pl = pl_t[u]
             gq = gqpool.tile([P, PASSES, UNIT, 4], BF16, tag="gq", name="gq%d" % u, align_bytes=64)
             xc = xcpool.tile([P, PASSES, UNIT], U32, tag="xc", name="xc%d" % u, align_bytes=64)
             xsc = xcpool.tile([P, PASSES, UNIT], U8, tag="xsc", name="xsc%d" % u, align_bytes=64)
@@ -174,8 +200,14 @@ def tile_groupedlinear_t_kernel(tc, x, ln_gamma, ln_beta, W, b, out):
                     scales=xsc[:, c2, :],
                     in_=gq[:, c2, :, :].rearrange("p n t -> p (n t)"),
                 )
+            xc_t[u] = xc
+            xsc_t[u] = xsc
 
+        def multiply_store(u):
+            g = u // UPG
+            q = u % UPG
             ysb = ypool.tile([P, OT, UNIT], F32, tag="y", name="y%d" % u)
+            yps = []
             for a in range(OT):
                 yp = psy.tile([P, UNIT], F32, tag="yp", name="yp%d_%d" % (u, a))
                 for c2 in range(PASSES):
@@ -183,17 +215,49 @@ def tile_groupedlinear_t_kernel(tc, x, ln_gamma, ln_beta, W, b, out):
                         out=yp[:],
                         lhsT=wc[:, g, c2, a * P:(a + 1) * P].bitcast(FP8X4),
                         lhsT_scale=ws[:, g, c2, a * P:(a + 1) * P],
-                        rhs=xc[:, c2, :].bitcast(FP8X4),
-                        rhs_scale=xsc[:, c2, :],
+                        rhs=xc_t[u][:, c2, :].bitcast(FP8X4),
+                        rhs_scale=xsc_t[u][:, c2, :],
                         start=(c2 == 0),
                         stop=(c2 == PASSES - 1),
                     )
+                yps.append(yp)
+            for a in range(OT):
                 bi = 64 + g * OT + a
-                nc.scalar.activation(out=ysb[:, a, :], in_=yp[:], func=ACT.Identity,
+                nc.scalar.activation(out=ysb[:, a, :], in_=yps[a][:], func=ACT.Identity,
                                      bias=cols[:, bi:bi + 1], scale=1.0)
             nc.sync.dma_start(
                 out=ov[g * O:(g + 1) * O, q * UNIT:(q + 1) * UNIT].rearrange("(t o) n -> o t n", t=OT),
                 in_=ysb[:],
             )
-            if q == 2 and g + 1 < G:
-                prep_w(g + 1)
+
+        for i in range(-1, UNITS + 2):
+            if live(i + XBUFS - 1):
+                load_x(i + XBUFS - 1)
+            if i >= 0 and i % UPG == 0 and i // UPG + 1 < G:
+                load_w(i // UPG + 1)
+            if live(i):
+                sqrt_(i)
+            if live(i - 2):
+                regroup_quantise(i - 2)
+            if (i - 1) in w_when:
+                w_quantise(*w_when[i - 1])
+            if live(i):
+                scalars(i)
+                for j in range(ROWT):
+                    if Z_ENGINE[j] != "s":
+                        zrow(i, j)
+            if live(i - 1):
+                pl_t[i - 1] = plpool.tile([P, CHUNKS, UNIT], BF16, tag="pl", name="pl%d" % (i - 1))
+            for c in range(CHUNKS):
+                if live(i - 1):
+                    bank(i - 1, c)
+                if c == S_Z_AFTER_BANK and live(i):
+                    for j in range(ROWT):
+                        if Z_ENGINE[j] == "s":
+                            zrow(i, j)
+            if live(i - 2):
+                multiply_store(i - 2)
+            if i in w_when:
+                w_transpose(*w_when[i])
+            if live(i + 1):
+                stats(i + 1)

@@ -1,6 +1,8 @@
 from contextlib import ExitStack
 
+import concourse.bass as bass
 import concourse.mybir as mybir
+import concourse.tile as tile
 from concourse.masks import make_identity
 
 F32 = mybir.dt.float32
@@ -17,19 +19,17 @@ K = 1024
 O = 256
 POS = 2048
 UNIT = 512
-UPG = POS // UNIT
-UNITS = G * UPG
+UNITS = G * POS // UNIT
 ROWT = UNIT // P
 CHUNKS = K // P
 PASSES = K // 512
 OT = O // P
 EPS = 1e-6
-XBUFS = 5
 
 FLOPS = 2 * G * POS * K * O
 
-Z_ENGINE = ("g", "g", "g", "s")
-S_Z_AFTER_BANK = 5
+Z_ENGINE = ("g", "g", "g", "v")
+VSTAT = 3
 
 
 def tile_groupedlinear_t_kernel(tc, x, ln_gamma, ln_beta, W, b, out):
@@ -39,7 +39,7 @@ def tile_groupedlinear_t_kernel(tc, x, ln_gamma, ln_beta, W, b, out):
 
     with ExitStack() as ctx:
         const = ctx.enter_context(tc.tile_pool(name="const", bufs=1))
-        xpool = ctx.enter_context(tc.tile_pool(name="xpool", bufs=XBUFS))
+        xpool = ctx.enter_context(tc.tile_pool(name="xpool", bufs=4))
         zpool = ctx.enter_context(tc.tile_pool(name="zpool", bufs=12))
         small = ctx.enter_context(tc.tile_pool(name="small", bufs=4))
         plpool = ctx.enter_context(tc.tile_pool(name="plpool", bufs=3))
@@ -47,24 +47,11 @@ def tile_groupedlinear_t_kernel(tc, x, ln_gamma, ln_beta, W, b, out):
         xcpool = ctx.enter_context(tc.tile_pool(name="xcpool", bufs=3))
         ypool = ctx.enter_context(tc.tile_pool(name="ypool", bufs=3))
         wstage = ctx.enter_context(tc.tile_pool(name="wstage", bufs=2))
+        junkp = ctx.enter_context(tc.tile_pool(name="junkp", bufs=2))
         pst = ctx.enter_context(tc.psum_pool(name="pst", bufs=6))
         psy = ctx.enter_context(tc.psum_pool(name="psy", bufs=2))
-        ctx.enter_context(tc.manual_schedule())
 
-        x_t = {}
-        mv_t = {}
-        std_t = {}
-        rstd_t = {}
-        negmu_t = {}
-        nmr_t = {}
-        z_t = {}
-        pl_t = {}
-        xc_t = {}
-        xsc_t = {}
-        wg_t = {}
-
-        def live(u):
-            return 0 <= u < UNITS
+        x_tiles = {}
 
         def load_x(u):
             xt = xpool.tile([P, ROWT, K], BF16, tag="x", name="xt%d" % u)
@@ -74,7 +61,15 @@ def tile_groupedlinear_t_kernel(tc, x, ln_gamma, ln_beta, W, b, out):
                     nc.sync.dma_start(out=xt[:, j, :], in_=rows[:, j, :])
             else:
                 nc.sync.dma_start(out=xt[:], in_=rows)
-            x_t[u] = xt
+            x_tiles[u] = xt
+
+        load_x(0)
+
+        prm = const.tile([P, P], BF16, name="prm")
+        nc.vector.memset(prm[:], 0.0)
+        nc.sync.dma_start(out=prm[0:32, :], in_=ln_gamma.rearrange("g (c p) -> (g c) p", p=P))
+        nc.sync.dma_start(out=prm[32:64, :], in_=ln_beta.rearrange("g (c p) -> (g c) p", p=P))
+        nc.sync.dma_start(out=prm[64:72, :], in_=b.rearrange("g (c p) -> (g c) p", p=P))
 
         w_raw = []
         for g in range(G):
@@ -84,108 +79,99 @@ def tile_groupedlinear_t_kernel(tc, x, ln_gamma, ln_beta, W, b, out):
         def load_w(g):
             nc.sync.dma_start(out=w_raw[g][:], in_=W[g].rearrange("(t o) k -> o t k", t=OT))
 
-        load_x(0)
-        prm = const.tile([P, P], BF16, name="prm")
-        nc.vector.memset(prm[:], 0.0)
-        eps_t = const.tile([P, 1], F32, name="eps_t")
-        nc.vector.memset(eps_t[:], EPS)
-        nc.sync.dma_start(out=prm[0:32, :], in_=ln_gamma.rearrange("g (c p) -> (g c) p", p=P))
-        nc.sync.dma_start(out=prm[32:64, :], in_=ln_beta.rearrange("g (c p) -> (g c) p", p=P))
-        nc.sync.dma_start(out=prm[64:72, :], in_=b.rearrange("g (c p) -> (g c) p", p=P))
         load_w(0)
-        for u in range(1, XBUFS - 2):
-            load_x(u)
+        load_x(1)
 
-        warm = const.tile([P, 1], F32, name="warm")
-        nc.scalar.activation(out=warm[:], in_=eps_t[:], func=ACT.Sqrt)
-
-        ident_b = const.tile([P, P], BF16, name="ident_b")
-        make_identity(nc, ident_b[:])
         ident_f = const.tile([P, P], F32, name="ident_f")
         make_identity(nc, ident_f[:])
+        ident_b = const.tile([P, P], BF16, name="ident_b")
+        make_identity(nc, ident_b[:])
+        eps_t = const.tile([P, 1], F32, name="eps_t")
+        nc.vector.memset(eps_t[:], EPS)
 
         prm_ps = pst.tile([P, P], BF16, tag="zt", name="prm_ps")
         nc.tensor.transpose(prm_ps[:], prm[:], ident_b[:])
         cols = const.tile([P, P], F32, name="cols")
-        nc.scalar.copy(out=cols[:], in_=prm_ps[:])
+        nc.vector.tensor_copy(out=cols[:], in_=prm_ps[:])
 
         wc = const.tile([P, G, PASSES, O], U32, name="wc", align_bytes=64)
         ws = const.tile([P, G, PASSES, O], U8, name="ws", align_bytes=64)
 
-        def w_transpose(g, c2):
-            wt = pst.tile([P, OT, 4, P], BF16, tag="zt", name="wt%d_%d" % (g, c2))
-            for a in range(OT):
-                for t in range(4):
-                    c = c2 * 4 + t
-                    nc.tensor.transpose(wt[:, a, t, :], w_raw[g][:, a, c * P:(c + 1) * P], ident_b[:])
-            wg = wstage.tile([P, OT, P, 4], BF16, tag="wg", name="wg%d_%d" % (g, c2), align_bytes=64)
-            nc.scalar.copy(out=wg[:], in_=wt[:].rearrange("p a t o -> p a o t"))
-            wg_t[(g, c2)] = wg
+        def prep_w(g):
+            for c2 in range(PASSES):
+                wt = pst.tile([P, OT, 4, P], BF16, tag="zt", name="wt%d_%d" % (g, c2))
+                for a in range(OT):
+                    for t in range(4):
+                        c = c2 * 4 + t
+                        nc.tensor.transpose(wt[:, a, t, :], w_raw[g][:, a, c * P:(c + 1) * P], ident_b[:])
+                wg = wstage.tile([P, OT, P, 4], BF16, tag="wg", name="wg%d_%d" % (g, c2), align_bytes=64)
+                nc.scalar.copy(out=wg[:], in_=wt[:].rearrange("p a t o -> p a o t"))
+                nc.vector.quantize_mx(
+                    out=wc[:, g, c2, :].bitcast(FP8X4),
+                    scales=ws[:, g, c2, :],
+                    in_=wg[:].rearrange("p a o t -> p (a o t)"),
+                )
 
-        def w_quantise(g, c2):
-            nc.vector.quantize_mx(
-                out=wc[:, g, c2, :].bitcast(FP8X4),
-                scales=ws[:, g, c2, :],
-                in_=wg_t[(g, c2)][:].rearrange("p a o t -> p (a o t)"),
-            )
+        prep_w(0)
 
-        w_when = {}
-        for g in range(G):
-            w_when[max(UPG * g - 2, -1)] = (g, 0)
-            w_when[max(UPG * g - 1, 0)] = (g, 1)
+        for u in range(UNITS):
+            g = u // (POS // UNIT)
+            q = u % (POS // UNIT)
+            if u + 2 < UNITS:
+                load_x(u + 2)
+            if q == 0 and g + 1 < G:
+                load_w(g + 1)
+            xt = x_tiles[u]
 
-        def stats(u):
-            xt = x_t[u]
-            st = small.tile([P, ROWT, 2, 6], F32, tag="st", name="st%d" % u)
-            mv = small.tile([P, ROWT, 2], F32, tag="mv", name="mv%d" % u)
-            for j in range(ROWT):
+            st = small.tile([P, VSTAT, 2, 6], F32, tag="st", name="st%d" % u)
+            mv = small.tile([P, VSTAT, 2], F32, tag="mv", name="mv%d" % u)
+            for j in range(VSTAT):
                 for h in range(2):
                     nc.vector.bn_stats(out=st[:, j, h, :], in_=xt[:, j, h * 512:(h + 1) * 512])
                 nc.vector.bn_aggr(out=mv[:, j, :], in_=st[:, j, :, :].rearrange("p h s -> p (h s)"))
-            mv_t[u] = mv
-
-        def sqrt_(u):
             std = small.tile([P, ROWT], F32, tag="std", name="std%d" % u)
-            nc.scalar.activation(out=std[:], in_=mv_t[u][:, :, 1], func=ACT.Sqrt, bias=eps_t[:], scale=1.0)
-            std_t[u] = std
-
-        def scalars(u):
+            nc.scalar.activation(out=std[:, 0:VSTAT], in_=mv[:, :, 1], func=ACT.Sqrt, bias=eps_t[:], scale=1.0)
+            negmean = {}
+            for j in range(VSTAT, ROWT):
+                junk = junkp.tile([P, K], BF16, tag="junk", name="junk%d_%d" % (u, j))
+                s1 = small.tile([P, 1], F32, tag="s1", name="s1_%d_%d" % (u, j))
+                nc.scalar.activation(out=junk[:], in_=xt[:, j, :], func=ACT.Identity, accum_out=s1[:])
+                nm = small.tile([P, 1], F32, tag="nm", name="nm%d_%d" % (u, j))
+                nc.scalar.activation(out=nm[:], in_=s1[:], func=ACT.Identity, scale=-1.0 / K)
+                junk2 = junkp.tile([P, K], BF16, tag="junk", name="junkb%d_%d" % (u, j))
+                ssd = small.tile([P, 1], F32, tag="ssd", name="ssd%d_%d" % (u, j))
+                nc.scalar.activation(out=junk2[:], in_=xt[:, j, :], func=ACT.Square, bias=nm[:], scale=1.0,
+                                     accum_out=ssd[:])
+                nc.scalar.activation(out=std[:, j:j + 1], in_=ssd[:], func=ACT.Sqrt, bias=eps_t[:], scale=1.0 / K)
+                negmean[j] = nm[:, 0:1]
             rstd = small.tile([P, ROWT], F32, tag="rstd", name="rstd%d" % u)
-            nc.vector.reciprocal(out=rstd[:], in_=std_t[u][:])
-            negmu = small.tile([P, ROWT], F32, tag="negmu", name="negmu%d" % u)
-            nc.vector.tensor_scalar(out=negmu[:], in0=mv_t[u][:, :, 0], scalar1=-1.0, scalar2=None, op0=ALU.mult)
-            nmr = small.tile([P, ROWT], F32, tag="nmr", name="nmr%d" % u)
-            nc.vector.tensor_tensor(out=nmr[:], in0=negmu[:], in1=rstd[:], op=ALU.mult)
-            rstd_t[u] = rstd
-            negmu_t[u] = negmu
-            nmr_t[u] = nmr
+            nc.vector.reciprocal(out=rstd[:], in_=std[:])
+            negmu = small.tile([P, VSTAT], F32, tag="negmu", name="negmu%d" % u)
+            nc.vector.tensor_scalar(out=negmu[:], in0=mv[:, :, 0], scalar1=-1.0, scalar2=None, op0=ALU.mult)
+            for j in range(VSTAT):
+                negmean[j] = negmu[:, j:j + 1]
 
-        def zrow(u, j):
-            z = zpool.tile([P, K], F32, tag="z", name="z%d_%d" % (u, j))
-            eng = Z_ENGINE[j]
-            xin = x_t[u][:, j, :]
-            if eng == "g":
-                nc.gpsimd.tensor_scalar(out=z[:], in0=xin, scalar1=negmu_t[u][:, j:j + 1],
-                                        scalar2=rstd_t[u][:, j:j + 1], op0=ALU.add, op1=ALU.mult)
-            elif eng == "v":
-                nc.vector.tensor_scalar(out=z[:], in0=xin, scalar1=negmu_t[u][:, j:j + 1],
-                                        scalar2=rstd_t[u][:, j:j + 1], op0=ALU.add, op1=ALU.mult)
-            else:
-                nc.scalar.activation(out=z[:], in_=xin, func=ACT.Identity,
-                                     scale=rstd_t[u][:, j:j + 1], bias=nmr_t[u][:, j:j + 1])
-            z_t[(u, j)] = z
-
-        def bank(u, c):
-            g = u // UPG
-            zp = pst.tile([P, UNIT], F32, tag="zt", name="zp%d_%d" % (u, c))
+            zs = []
             for j in range(ROWT):
-                nc.tensor.transpose(zp[:, j * P:(j + 1) * P], z_t[(u, j)][:, c * P:(c + 1) * P], ident_f[:])
-            gi = g * CHUNKS + c
-            nc.scalar.activation(out=pl_t[u][:, c, :], in_=zp[:], func=ACT.Identity,
-                                 scale=cols[:, gi:gi + 1], bias=cols[:, 32 + gi:33 + gi])
+                z = zpool.tile([P, K], F32, tag="z", name="z%d_%d" % (u, j))
+                eng = Z_ENGINE[j]
+                if eng == "g":
+                    nc.gpsimd.tensor_scalar(out=z[:], in0=xt[:, j, :], scalar1=negmean[j],
+                                            scalar2=rstd[:, j:j + 1], op0=ALU.add, op1=ALU.mult)
+                else:
+                    nc.vector.tensor_scalar(out=z[:], in0=xt[:, j, :], scalar1=negmean[j],
+                                            scalar2=rstd[:, j:j + 1], op0=ALU.add, op1=ALU.mult)
+                zs.append(z)
 
-        def regroup_quantise(u):
-            pl = pl_t[u]
+            pl = plpool.tile([P, CHUNKS, UNIT], BF16, tag="pl", name="pl%d" % u)
+            for c in range(CHUNKS):
+                zp = pst.tile([P, UNIT], F32, tag="zt", name="zp%d_%d" % (u, c))
+                for j in range(ROWT):
+                    nc.tensor.transpose(zp[:, j * P:(j + 1) * P], zs[j][:, c * P:(c + 1) * P], ident_f[:])
+                gi = g * CHUNKS + c
+                nc.scalar.activation(out=pl[:, c, :], in_=zp[:], func=ACT.Identity,
+                                     scale=cols[:, gi:gi + 1], bias=cols[:, 32 + gi:33 + gi])
+
             gq = gqpool.tile([P, PASSES, UNIT, 4], BF16, tag="gq", name="gq%d" % u, align_bytes=64)
             xc = xcpool.tile([P, PASSES, UNIT], U32, tag="xc", name="xc%d" % u, align_bytes=64)
             xsc = xcpool.tile([P, PASSES, UNIT], U8, tag="xsc", name="xsc%d" % u, align_bytes=64)
@@ -200,14 +186,8 @@ def tile_groupedlinear_t_kernel(tc, x, ln_gamma, ln_beta, W, b, out):
                     scales=xsc[:, c2, :],
                     in_=gq[:, c2, :, :].rearrange("p n t -> p (n t)"),
                 )
-            xc_t[u] = xc
-            xsc_t[u] = xsc
 
-        def multiply_store(u):
-            g = u // UPG
-            q = u % UPG
             ysb = ypool.tile([P, OT, UNIT], F32, tag="y", name="y%d" % u)
-            yps = []
             for a in range(OT):
                 yp = psy.tile([P, UNIT], F32, tag="yp", name="yp%d_%d" % (u, a))
                 for c2 in range(PASSES):
@@ -215,49 +195,17 @@ def tile_groupedlinear_t_kernel(tc, x, ln_gamma, ln_beta, W, b, out):
                         out=yp[:],
                         lhsT=wc[:, g, c2, a * P:(a + 1) * P].bitcast(FP8X4),
                         lhsT_scale=ws[:, g, c2, a * P:(a + 1) * P],
-                        rhs=xc_t[u][:, c2, :].bitcast(FP8X4),
-                        rhs_scale=xsc_t[u][:, c2, :],
+                        rhs=xc[:, c2, :].bitcast(FP8X4),
+                        rhs_scale=xsc[:, c2, :],
                         start=(c2 == 0),
                         stop=(c2 == PASSES - 1),
                     )
-                yps.append(yp)
-            for a in range(OT):
                 bi = 64 + g * OT + a
-                nc.scalar.activation(out=ysb[:, a, :], in_=yps[a][:], func=ACT.Identity,
+                nc.scalar.activation(out=ysb[:, a, :], in_=yp[:], func=ACT.Identity,
                                      bias=cols[:, bi:bi + 1], scale=1.0)
             nc.sync.dma_start(
                 out=ov[g * O:(g + 1) * O, q * UNIT:(q + 1) * UNIT].rearrange("(t o) n -> o t n", t=OT),
                 in_=ysb[:],
             )
-
-        for i in range(-1, UNITS + 2):
-            if live(i + XBUFS - 1):
-                load_x(i + XBUFS - 1)
-            if i >= 0 and i % UPG == 0 and i // UPG + 1 < G:
-                load_w(i // UPG + 1)
-            if live(i):
-                sqrt_(i)
-            if live(i - 2):
-                regroup_quantise(i - 2)
-            if (i - 1) in w_when:
-                w_quantise(*w_when[i - 1])
-            if live(i):
-                scalars(i)
-                for j in range(ROWT):
-                    if Z_ENGINE[j] != "s":
-                        zrow(i, j)
-            if live(i - 1):
-                pl_t[i - 1] = plpool.tile([P, CHUNKS, UNIT], BF16, tag="pl", name="pl%d" % (i - 1))
-            for c in range(CHUNKS):
-                if live(i - 1):
-                    bank(i - 1, c)
-                if c == S_Z_AFTER_BANK and live(i):
-                    for j in range(ROWT):
-                        if Z_ENGINE[j] == "s":
-                            zrow(i, j)
-            if live(i - 2):
-                multiply_store(i - 2)
-            if i in w_when:
-                w_transpose(*w_when[i])
-            if live(i + 1):
-                stats(i + 1)
+            if q == 2 and g + 1 < G:
+                prep_w(g + 1)

@@ -1,8 +1,6 @@
 from contextlib import ExitStack
 
-import concourse.bass as bass
 import concourse.mybir as mybir
-import concourse.tile as tile
 from concourse.masks import make_identity
 
 F32 = mybir.dt.float32
@@ -19,17 +17,19 @@ K = 1024
 O = 256
 POS = 2048
 UNIT = 512
-UNITS = G * POS // UNIT
+UPG = POS // UNIT
+UNITS = G * UPG
 ROWT = UNIT // P
 CHUNKS = K // P
 PASSES = K // 512
 OT = O // P
 EPS = 1e-6
+XBUFS = 5
 
 FLOPS = 2 * G * POS * K * O
 
-Z_ENGINE = ("g", "g", "g", "v")
-VSTAT = 3
+Z_ENGINE = ("g", "g", "g", "s")
+Z_LAST = ("v", "v", "v", "v")
 
 
 def tile_groupedlinear_t_kernel(tc, x, ln_gamma, ln_beta, W, b, out):
@@ -39,7 +39,7 @@ def tile_groupedlinear_t_kernel(tc, x, ln_gamma, ln_beta, W, b, out):
 
     with ExitStack() as ctx:
         const = ctx.enter_context(tc.tile_pool(name="const", bufs=1))
-        xpool = ctx.enter_context(tc.tile_pool(name="xpool", bufs=4))
+        xpool = ctx.enter_context(tc.tile_pool(name="xpool", bufs=XBUFS))
         zpool = ctx.enter_context(tc.tile_pool(name="zpool", bufs=12))
         small = ctx.enter_context(tc.tile_pool(name="small", bufs=4))
         plpool = ctx.enter_context(tc.tile_pool(name="plpool", bufs=3))
@@ -47,11 +47,24 @@ def tile_groupedlinear_t_kernel(tc, x, ln_gamma, ln_beta, W, b, out):
         xcpool = ctx.enter_context(tc.tile_pool(name="xcpool", bufs=3))
         ypool = ctx.enter_context(tc.tile_pool(name="ypool", bufs=3))
         wstage = ctx.enter_context(tc.tile_pool(name="wstage", bufs=2))
-        junkp = ctx.enter_context(tc.tile_pool(name="junkp", bufs=2))
         pst = ctx.enter_context(tc.psum_pool(name="pst", bufs=6))
         psy = ctx.enter_context(tc.psum_pool(name="psy", bufs=2))
+        ctx.enter_context(tc.manual_schedule())
 
-        x_tiles = {}
+        x_t = {}
+        mv_t = {}
+        std_t = {}
+        rstd_t = {}
+        negmu_t = {}
+        nmr_t = {}
+        z_t = {}
+        pl_t = {}
+        xc_t = {}
+        xsc_t = {}
+        wg_t = {}
+
+        def live(u):
+            return 0 <= u < UNITS
 
         def load_x(u):
             xt = xpool.tile([P, ROWT, K], BF16, tag="x", name="xt%d" % u)
@@ -61,15 +74,7 @@ def tile_groupedlinear_t_kernel(tc, x, ln_gamma, ln_beta, W, b, out):
                     nc.sync.dma_start(out=xt[:, j, :], in_=rows[:, j, :])
             else:
                 nc.sync.dma_start(out=xt[:], in_=rows)
-            x_tiles[u] = xt
-
-        load_x(0)
-
-        prm = const.tile([P, P], BF16, name="prm")
-        nc.vector.memset(prm[:], 0.0)
-        nc.sync.dma_start(out=prm[0:32, :], in_=ln_gamma.rearrange("g (c p) -> (g c) p", p=P))
-        nc.sync.dma_start(out=prm[32:64, :], in_=ln_beta.rearrange("g (c p) -> (g c) p", p=P))
-        nc.sync.dma_start(out=prm[64:72, :], in_=b.rearrange("g (c p) -> (g c) p", p=P))
+            x_t[u] = xt
 
         w_raw = []
         for g in range(G):
@@ -79,133 +84,209 @@ def tile_groupedlinear_t_kernel(tc, x, ln_gamma, ln_beta, W, b, out):
         def load_w(g):
             nc.sync.dma_start(out=w_raw[g][:], in_=W[g].rearrange("(t o) k -> o t k", t=OT))
 
-        load_w(0)
-        load_x(1)
-
-        ident_f = const.tile([P, P], F32, name="ident_f")
-        make_identity(nc, ident_f[:])
-        ident_b = const.tile([P, P], BF16, name="ident_b")
-        make_identity(nc, ident_b[:])
+        load_x(0)
+        prm = const.tile([P, P], BF16, name="prm")
+        nc.vector.memset(prm[:], 0.0)
         eps_t = const.tile([P, 1], F32, name="eps_t")
         nc.vector.memset(eps_t[:], EPS)
+        nc.sync.dma_start(out=prm[0:32, :], in_=ln_gamma.rearrange("g (c p) -> (g c) p", p=P))
+        nc.sync.dma_start(out=prm[32:64, :], in_=ln_beta.rearrange("g (c p) -> (g c) p", p=P))
+        nc.sync.dma_start(out=prm[64:72, :], in_=b.rearrange("g (c p) -> (g c) p", p=P))
+        load_w(0)
+        for u in range(1, XBUFS - 2):
+            load_x(u)
+
+        warm = const.tile([P, 1], F32, name="warm")
+        nc.scalar.activation(out=warm[:], in_=eps_t[:], func=ACT.Sqrt)
+
+        ident_b = const.tile([P, P], BF16, name="ident_b")
+        make_identity(nc, ident_b[:])
+        ident_f = const.tile([P, P], F32, name="ident_f")
+        make_identity(nc, ident_f[:])
 
         prm_ps = pst.tile([P, P], BF16, tag="zt", name="prm_ps")
         nc.tensor.transpose(prm_ps[:], prm[:], ident_b[:])
         cols = const.tile([P, P], F32, name="cols")
-        nc.vector.tensor_copy(out=cols[:], in_=prm_ps[:])
+        nc.scalar.copy(out=cols[:], in_=prm_ps[:])
 
         wc = const.tile([P, G, PASSES, O], U32, name="wc", align_bytes=64)
         ws = const.tile([P, G, PASSES, O], U8, name="ws", align_bytes=64)
 
-        def prep_w(g):
-            for c2 in range(PASSES):
-                wt = pst.tile([P, OT, 4, P], BF16, tag="zt", name="wt%d_%d" % (g, c2))
-                for a in range(OT):
-                    for t in range(4):
-                        c = c2 * 4 + t
-                        nc.tensor.transpose(wt[:, a, t, :], w_raw[g][:, a, c * P:(c + 1) * P], ident_b[:])
-                wg = wstage.tile([P, OT, P, 4], BF16, tag="wg", name="wg%d_%d" % (g, c2), align_bytes=64)
-                nc.scalar.copy(out=wg[:], in_=wt[:].rearrange("p a t o -> p a o t"))
-                nc.vector.quantize_mx(
-                    out=wc[:, g, c2, :].bitcast(FP8X4),
-                    scales=ws[:, g, c2, :],
-                    in_=wg[:].rearrange("p a o t -> p (a o t)"),
-                )
+        def w_transpose(g, c2):
+            wt = pst.tile([P, OT, 4, P], BF16, tag="zt", name="wt%d_%d" % (g, c2))
+            for a in range(OT):
+                for t in range(4):
+                    c = c2 * 4 + t
+                    nc.tensor.transpose(wt[:, a, t, :], w_raw[g][:, a, c * P:(c + 1) * P], ident_b[:])
+            wg = wstage.tile([P, OT, P, 4], BF16, tag="wg", name="wg%d_%d" % (g, c2), align_bytes=64)
+            nc.scalar.copy(out=wg[:], in_=wt[:].rearrange("p a t o -> p a o t"))
+            wg_t[(g, c2)] = wg
 
-        prep_w(0)
+        def w_quantise(g, c2):
+            nc.vector.quantize_mx(
+                out=wc[:, g, c2, :].bitcast(FP8X4),
+                scales=ws[:, g, c2, :],
+                in_=wg_t[(g, c2)][:].rearrange("p a o t -> p (a o t)"),
+            )
 
-        for u in range(UNITS):
-            g = u // (POS // UNIT)
-            q = u % (POS // UNIT)
-            if u + 2 < UNITS:
-                load_x(u + 2)
-            if q == 0 and g + 1 < G:
-                load_w(g + 1)
-            xt = x_tiles[u]
+        w_when = {}
+        for g in range(G):
+            w_when[max(UPG * g - 2, -1)] = (g, 0)
+            w_when[max(UPG * g - 1, 0)] = (g, 1)
 
-            st = small.tile([P, VSTAT, 2, 6], F32, tag="st", name="st%d" % u)
-            mv = small.tile([P, VSTAT, 2], F32, tag="mv", name="mv%d" % u)
-            for j in range(VSTAT):
-                for h in range(2):
-                    nc.vector.bn_stats(out=st[:, j, h, :], in_=xt[:, j, h * 512:(h + 1) * 512])
-                nc.vector.bn_aggr(out=mv[:, j, :], in_=st[:, j, :, :].rearrange("p h s -> p (h s)"))
+        st_t = {}
+
+        def bn(u, j, h):
+            if u not in st_t:
+                st_t[u] = small.tile([P, ROWT, 2, 6], F32, tag="st", name="st%d" % u)
+                mv_t[u] = small.tile([P, ROWT, 2], F32, tag="mv", name="mv%d" % u)
+            nc.vector.bn_stats(out=st_t[u][:, j, h, :], in_=x_t[u][:, j, h * 512:(h + 1) * 512])
+
+        def aggr(u, j):
+            nc.vector.bn_aggr(out=mv_t[u][:, j, :], in_=st_t[u][:, j, :, :].rearrange("p h s -> p (h s)"))
+
+        def sqrt_(u):
             std = small.tile([P, ROWT], F32, tag="std", name="std%d" % u)
-            nc.scalar.activation(out=std[:, 0:VSTAT], in_=mv[:, :, 1], func=ACT.Sqrt, bias=eps_t[:], scale=1.0)
-            negmean = {}
-            for j in range(VSTAT, ROWT):
-                junk = junkp.tile([P, K], BF16, tag="junk", name="junk%d_%d" % (u, j))
-                s1 = small.tile([P, 1], F32, tag="s1", name="s1_%d_%d" % (u, j))
-                nc.scalar.activation(out=junk[:], in_=xt[:, j, :], func=ACT.Identity, accum_out=s1[:])
-                nm = small.tile([P, 1], F32, tag="nm", name="nm%d_%d" % (u, j))
-                nc.scalar.activation(out=nm[:], in_=s1[:], func=ACT.Identity, scale=-1.0 / K)
-                junk2 = junkp.tile([P, K], BF16, tag="junk", name="junkb%d_%d" % (u, j))
-                ssd = small.tile([P, 1], F32, tag="ssd", name="ssd%d_%d" % (u, j))
-                nc.scalar.activation(out=junk2[:], in_=xt[:, j, :], func=ACT.Square, bias=nm[:], scale=1.0,
-                                     accum_out=ssd[:])
-                nc.scalar.activation(out=std[:, j:j + 1], in_=ssd[:], func=ACT.Sqrt, bias=eps_t[:], scale=1.0 / K)
-                negmean[j] = nm[:, 0:1]
-            rstd = small.tile([P, ROWT], F32, tag="rstd", name="rstd%d" % u)
-            nc.vector.reciprocal(out=rstd[:], in_=std[:])
-            negmu = small.tile([P, VSTAT], F32, tag="negmu", name="negmu%d" % u)
-            nc.vector.tensor_scalar(out=negmu[:], in0=mv[:, :, 0], scalar1=-1.0, scalar2=None, op0=ALU.mult)
-            for j in range(VSTAT):
-                negmean[j] = negmu[:, j:j + 1]
+            nc.scalar.activation(out=std[:], in_=mv_t[u][:, :, 1], func=ACT.Sqrt, bias=eps_t[:], scale=1.0)
+            std_t[u] = std
 
-            zs = []
+        def recip(u):
+            rstd_t[u] = small.tile([P, ROWT], F32, tag="rstd", name="rstd%d" % u)
+            nc.vector.reciprocal(out=rstd_t[u][:], in_=std_t[u][:])
+
+        def negmean(u):
+            negmu_t[u] = small.tile([P, ROWT], F32, tag="negmu", name="negmu%d" % u)
+            nc.vector.tensor_scalar(out=negmu_t[u][:], in0=mv_t[u][:, :, 0], scalar1=-1.0, scalar2=None, op0=ALU.mult)
+
+        def negmean_rstd(u):
+            nmr_t[u] = small.tile([P, ROWT], F32, tag="nmr", name="nmr%d" % u)
+            nc.vector.tensor_tensor(out=nmr_t[u][:], in0=negmu_t[u][:], in1=rstd_t[u][:], op=ALU.mult)
+
+        def zrow(u, j, eng):
+            z = zpool.tile([P, K], F32, tag="z", name="z%d_%d" % (u, j))
+            xin = x_t[u][:, j, :]
+            if eng == "g":
+                nc.gpsimd.tensor_scalar(out=z[:], in0=xin, scalar1=negmu_t[u][:, j:j + 1],
+                                        scalar2=rstd_t[u][:, j:j + 1], op0=ALU.add, op1=ALU.mult)
+            elif eng == "v":
+                nc.vector.tensor_scalar(out=z[:], in0=xin, scalar1=negmu_t[u][:, j:j + 1],
+                                        scalar2=rstd_t[u][:, j:j + 1], op0=ALU.add, op1=ALU.mult)
+            else:
+                nc.scalar.activation(out=z[:], in_=xin, func=ACT.Identity,
+                                     scale=rstd_t[u][:, j:j + 1], bias=nmr_t[u][:, j:j + 1])
+            z_t[(u, j)] = z
+
+        def bank(u, c):
+            g = u // UPG
+            zp = pst.tile([P, UNIT], F32, tag="zt", name="zp%d_%d" % (u, c))
             for j in range(ROWT):
-                z = zpool.tile([P, K], F32, tag="z", name="z%d_%d" % (u, j))
-                eng = Z_ENGINE[j]
-                if eng == "g":
-                    nc.gpsimd.tensor_scalar(out=z[:], in0=xt[:, j, :], scalar1=negmean[j],
-                                            scalar2=rstd[:, j:j + 1], op0=ALU.add, op1=ALU.mult)
-                else:
-                    nc.vector.tensor_scalar(out=z[:], in0=xt[:, j, :], scalar1=negmean[j],
-                                            scalar2=rstd[:, j:j + 1], op0=ALU.add, op1=ALU.mult)
-                zs.append(z)
+                nc.tensor.transpose(zp[:, j * P:(j + 1) * P], z_t[(u, j)][:, c * P:(c + 1) * P], ident_f[:])
+            gi = g * CHUNKS + c
+            nc.scalar.activation(out=pl_t[u][:, c, :], in_=zp[:], func=ACT.Identity,
+                                 scale=cols[:, gi:gi + 1], bias=cols[:, 32 + gi:33 + gi])
 
-            pl = plpool.tile([P, CHUNKS, UNIT], BF16, tag="pl", name="pl%d" % u)
-            for c in range(CHUNKS):
-                zp = pst.tile([P, UNIT], F32, tag="zt", name="zp%d_%d" % (u, c))
-                for j in range(ROWT):
-                    nc.tensor.transpose(zp[:, j * P:(j + 1) * P], zs[j][:, c * P:(c + 1) * P], ident_f[:])
-                gi = g * CHUNKS + c
-                nc.scalar.activation(out=pl[:, c, :], in_=zp[:], func=ACT.Identity,
-                                     scale=cols[:, gi:gi + 1], bias=cols[:, 32 + gi:33 + gi])
+        gq_t = {}
 
-            gq = gqpool.tile([P, PASSES, UNIT, 4], BF16, tag="gq", name="gq%d" % u, align_bytes=64)
-            xc = xcpool.tile([P, PASSES, UNIT], U32, tag="xc", name="xc%d" % u, align_bytes=64)
-            xsc = xcpool.tile([P, PASSES, UNIT], U8, tag="xsc", name="xsc%d" % u, align_bytes=64)
-            for c2 in range(PASSES):
-                nc.vector.tensor_copy(
-                    out=gq[:, c2, :, :].rearrange("p (c i) t -> p c t i", i=4),
-                    in_=pl[:, c2 * 4:(c2 + 1) * 4, :].rearrange("p t (c i) -> p c t i", i=4),
-                )
-            for c2 in range(PASSES):
-                nc.vector.quantize_mx(
-                    out=xc[:, c2, :].bitcast(FP8X4),
-                    scales=xsc[:, c2, :],
-                    in_=gq[:, c2, :, :].rearrange("p n t -> p (n t)"),
-                )
+        def regroup(u, c2):
+            if u not in gq_t:
+                gq_t[u] = gqpool.tile([P, PASSES, UNIT, 4], BF16, tag="gq", name="gq%d" % u, align_bytes=64)
+            nc.vector.tensor_copy(
+                out=gq_t[u][:, c2, :, :].rearrange("p (c i) t -> p c t i", i=4),
+                in_=pl_t[u][:, c2 * 4:(c2 + 1) * 4, :].rearrange("p t (c i) -> p c t i", i=4),
+            )
 
+        def quantise(u, c2):
+            if u not in xc_t:
+                xc_t[u] = xcpool.tile([P, PASSES, UNIT], U32, tag="xc", name="xc%d" % u, align_bytes=64)
+                xsc_t[u] = xcpool.tile([P, PASSES, UNIT], U8, tag="xsc", name="xsc%d" % u, align_bytes=64)
+            nc.vector.quantize_mx(
+                out=xc_t[u][:, c2, :].bitcast(FP8X4),
+                scales=xsc_t[u][:, c2, :],
+                in_=gq_t[u][:, c2, :, :].rearrange("p n t -> p (n t)"),
+            )
+
+        def multiply_store(u):
+            g = u // UPG
+            q = u % UPG
+            last = u == UNITS - 1
             ysb = ypool.tile([P, OT, UNIT], F32, tag="y", name="y%d" % u)
+            yps = []
             for a in range(OT):
                 yp = psy.tile([P, UNIT], F32, tag="yp", name="yp%d_%d" % (u, a))
-                for c2 in range(PASSES):
+                yps.append(yp)
+            for c2 in range(PASSES):
+                for a in range(OT):
                     nc.tensor.matmul_mx(
-                        out=yp[:],
+                        out=yps[a][:],
                         lhsT=wc[:, g, c2, a * P:(a + 1) * P].bitcast(FP8X4),
                         lhsT_scale=ws[:, g, c2, a * P:(a + 1) * P],
-                        rhs=xc[:, c2, :].bitcast(FP8X4),
-                        rhs_scale=xsc[:, c2, :],
+                        rhs=xc_t[u][:, c2, :].bitcast(FP8X4),
+                        rhs_scale=xsc_t[u][:, c2, :],
                         start=(c2 == 0),
                         stop=(c2 == PASSES - 1),
                     )
+            dst = ov[g * O:(g + 1) * O, q * UNIT:(q + 1) * UNIT].rearrange("(t o) n -> o t n", t=OT)
+            for a in range(OT):
                 bi = 64 + g * OT + a
-                nc.scalar.activation(out=ysb[:, a, :], in_=yp[:], func=ACT.Identity,
-                                     bias=cols[:, bi:bi + 1], scale=1.0)
-            nc.sync.dma_start(
-                out=ov[g * O:(g + 1) * O, q * UNIT:(q + 1) * UNIT].rearrange("(t o) n -> o t n", t=OT),
-                in_=ysb[:],
-            )
-            if q == 2 and g + 1 < G:
-                prep_w(g + 1)
+                if last and a == 1:
+                    nc.vector.tensor_scalar(out=ysb[:, a, :], in0=yps[a][:], scalar1=cols[:, bi:bi + 1],
+                                            scalar2=None, op0=ALU.add)
+                else:
+                    nc.scalar.activation(out=ysb[:, a, :], in_=yps[a][:], func=ACT.Identity,
+                                         bias=cols[:, bi:bi + 1], scale=1.0)
+                if last:
+                    nc.sync.dma_start(out=dst[:, a, :], in_=ysb[:, a, :])
+            if not last:
+                nc.sync.dma_start(out=dst, in_=ysb[:])
+
+        for i in range(-1, UNITS + 2):
+            if live(i + XBUFS - 1):
+                load_x(i + XBUFS - 1)
+            if i >= 0 and i % UPG == 0 and i // UPG + 1 < G:
+                load_w(i // UPG + 1)
+            if live(i):
+                sqrt_(i)
+            last_a = i - 2 == UNITS - 1
+            if live(i - 2):
+                regroup(i - 2, 0)
+                if not last_a:
+                    regroup(i - 2, 1)
+            if live(i):
+                recip(i)
+            if live(i - 2):
+                quantise(i - 2, 0)
+            if (i - 1) in w_when:
+                w_quantise(*w_when[i - 1])
+            if last_a:
+                regroup(i - 2, 1)
+            if live(i - 2):
+                quantise(i - 2, 1)
+            z_eng = Z_LAST if i == UNITS - 1 else Z_ENGINE
+            if live(i):
+                negmean(i)
+                for j in range(ROWT):
+                    if z_eng[j] != "s":
+                        zrow(i, j, z_eng[j])
+            if live(i + 1):
+                bn(i + 1, 0, 0)
+            if live(i) and "s" in z_eng:
+                negmean_rstd(i)
+            if live(i - 1):
+                pl_t[i - 1] = plpool.tile([P, CHUNKS, UNIT], BF16, tag="pl", name="pl%d" % (i - 1))
+                for c in range(CHUNKS):
+                    bank(i - 1, c)
+            if live(i):
+                for j in range(ROWT):
+                    if z_eng[j] == "s":
+                        zrow(i, j, "s")
+            if live(i - 2):
+                multiply_store(i - 2)
+            if i in w_when:
+                w_transpose(*w_when[i])
+            if live(i + 1):
+                bn(i + 1, 0, 1)
+                for j in range(1, ROWT):
+                    bn(i + 1, j, 0)
+                    bn(i + 1, j, 1)
+                for j in range(ROWT):
+                    aggr(i + 1, j)

@@ -30,6 +30,7 @@ FLOPS = 2 * G * POS * K * O
 
 Z_ENGINE = ("g", "g", "g", "s")
 Z_LAST = ("v", "v", "v", "v")
+S_COLS = 64
 
 
 def tile_groupedlinear_t_kernel(tc, x, ln_gamma, ln_beta, W, b, out):
@@ -156,11 +157,15 @@ def tile_groupedlinear_t_kernel(tc, x, ln_gamma, ln_beta, W, b, out):
 
         def negmean(u):
             negmu_t[u] = small.tile([P, ROWT], F32, tag="negmu", name="negmu%d" % u)
-            nc.vector.tensor_scalar(out=negmu_t[u][:], in0=mv_t[u][:, :, 0], scalar1=-1.0, scalar2=None, op0=ALU.mult)
+            nc.gpsimd.tensor_scalar(out=negmu_t[u][:], in0=mv_t[u][:, :, 0], scalar1=-1.0, scalar2=0.0,
+                                    op0=ALU.mult, op1=ALU.add)
 
         def negmean_rstd(u):
             nmr_t[u] = small.tile([P, ROWT], F32, tag="nmr", name="nmr%d" % u)
-            nc.vector.tensor_tensor(out=nmr_t[u][:], in0=negmu_t[u][:], in1=rstd_t[u][:], op=ALU.mult)
+            for j in range(ROWT):
+                if Z_ENGINE[j] == "s":
+                    nc.scalar.activation(out=nmr_t[u][:, j:j + 1], in_=negmu_t[u][:, j:j + 1], func=ACT.Copy,
+                                         scale=rstd_t[u][:, j:j + 1])
 
         def zrow(u, j, eng):
             z = zpool.tile([P, K], F32, tag="z", name="z%d_%d" % (u, j))
@@ -187,13 +192,15 @@ def tile_groupedlinear_t_kernel(tc, x, ln_gamma, ln_beta, W, b, out):
 
         gq_t = {}
 
-        def regroup(u, c2):
+        def regroup(u, c2, eng, n0, n1):
             if u not in gq_t:
                 gq_t[u] = gqpool.tile([P, PASSES, UNIT, 4], BF16, tag="gq", name="gq%d" % u, align_bytes=64)
-            nc.vector.tensor_copy(
-                out=gq_t[u][:, c2, :, :].rearrange("p (c i) t -> p c t i", i=4),
-                in_=pl_t[u][:, c2 * 4:(c2 + 1) * 4, :].rearrange("p t (c i) -> p c t i", i=4),
-            )
+            dst = gq_t[u][:, c2, n0:n1, :].rearrange("p (c i) t -> p c t i", i=4)
+            src = pl_t[u][:, c2 * 4:(c2 + 1) * 4, n0:n1].rearrange("p t (c i) -> p c t i", i=4)
+            if eng == "v":
+                nc.vector.tensor_copy(out=dst, in_=src)
+            else:
+                nc.scalar.copy(out=dst, in_=src)
 
         def quantise(u, c2):
             if u not in xc_t:
@@ -246,46 +253,45 @@ def tile_groupedlinear_t_kernel(tc, x, ln_gamma, ln_beta, W, b, out):
                 load_w(i // UPG + 1)
             if live(i):
                 sqrt_(i)
+                negmean(i)
             last_a = i - 2 == UNITS - 1
             if live(i - 2):
-                regroup(i - 2, 0)
+                regroup(i - 2, 0, "v", 0, UNIT)
                 if not last_a:
-                    regroup(i - 2, 1)
-            if live(i):
-                recip(i)
-            if live(i - 2):
+                    regroup(i - 2, 1, "v", 0, UNIT - S_COLS)
                 quantise(i - 2, 0)
             if (i - 1) in w_when:
                 w_quantise(*w_when[i - 1])
             if last_a:
-                regroup(i - 2, 1)
+                regroup(i - 2, 1, "v", 0, UNIT)
             if live(i - 2):
                 quantise(i - 2, 1)
             z_eng = Z_LAST if i == UNITS - 1 else Z_ENGINE
             if live(i):
-                negmean(i)
+                recip(i)
                 for j in range(ROWT):
                     if z_eng[j] != "s":
                         zrow(i, j, z_eng[j])
-            if live(i + 1):
-                bn(i + 1, 0, 0)
-            if live(i) and "s" in z_eng:
-                negmean_rstd(i)
             if live(i - 1):
                 pl_t[i - 1] = plpool.tile([P, CHUNKS, UNIT], BF16, tag="pl", name="pl%d" % (i - 1))
                 for c in range(CHUNKS):
                     bank(i - 1, c)
+                    if c == 5 and live(i) and "s" in z_eng:
+                        negmean_rstd(i)
+            elif live(i) and "s" in z_eng:
+                negmean_rstd(i)
             if live(i):
                 for j in range(ROWT):
                     if z_eng[j] == "s":
                         zrow(i, j, "s")
+            if live(i - 1) and i - 1 != UNITS - 1:
+                regroup(i - 1, 1, "s", UNIT - S_COLS, UNIT)
             if live(i - 2):
                 multiply_store(i - 2)
             if i in w_when:
                 w_transpose(*w_when[i])
             if live(i + 1):
-                bn(i + 1, 0, 1)
-                for j in range(1, ROWT):
+                for j in range(ROWT):
                     bn(i + 1, j, 0)
                     bn(i + 1, j, 1)
                 for j in range(ROWT):

@@ -157,8 +157,7 @@ def tile_groupedlinear_t_kernel(tc, x, ln_gamma, ln_beta, W, b, out):
 
         def negmean(u):
             negmu_t[u] = small.tile([P, ROWT], F32, tag="negmu", name="negmu%d" % u)
-            nc.gpsimd.tensor_scalar(out=negmu_t[u][:], in0=mv_t[u][:, :, 0], scalar1=-1.0, scalar2=0.0,
-                                    op0=ALU.mult, op1=ALU.add)
+            nc.scalar.activation(out=negmu_t[u][:], in_=mv_t[u][:, :, 0], func=ACT.Copy, scale=-1.0)
 
         def negmean_rstd(u):
             nmr_t[u] = small.tile([P, ROWT], F32, tag="nmr", name="nmr%d" % u)
@@ -264,11 +263,12 @@ def tile_groupedlinear_t_kernel(tc, x, ln_gamma, ln_beta, W, b, out):
                 w_quantise(*w_when[i - 1])
             if last_a:
                 regroup(i - 2, 1, "v", 0, UNIT)
+            if live(i):
+                recip(i)
             if live(i - 2):
                 quantise(i - 2, 1)
             z_eng = Z_LAST if i == UNITS - 1 else Z_ENGINE
             if live(i):
-                recip(i)
                 for j in range(ROWT):
                     if z_eng[j] != "s":
                         zrow(i, j, z_eng[j])

from contextlib import ExitStack

import concourse.mybir as mybir
from concourse.masks import make_identity

F32 = mybir.dt.float32
BF16 = mybir.dt.bfloat16
U32 = mybir.dt.uint32
U8 = mybir.dt.uint8
FP8X4 = mybir.dt.float8_e4m3fn_x4
ALU = mybir.AluOpType
ACT = mybir.ActivationFunctionType

P = 128
G = 4
K = 1024
O = 256
POS = 2048
UNIT = 512
UPG = POS // UNIT
UNITS = G * UPG
ROWT = UNIT // P
CHUNKS = K // P
PASSES = K // 512
OT = O // P
EPS = 1e-6
XBUFS = 5

FLOPS = 2 * G * POS * K * O

Z_ENGINE = ("g", "g", "g", "s")
Z_LAST = ("v", "v", "v", "v")
S_COLS = 64


def tile_groupedlinear_t_kernel(tc, x, ln_gamma, ln_beta, W, b, out):
    nc = tc.nc
    xv = x.rearrange("a (h b) c d -> (a h) (b c d)", h=2)
    ov = out.rearrange("o a b c -> o (a b c)")

    with ExitStack() as ctx:
        const = ctx.enter_context(tc.tile_pool(name="const", bufs=1))
        xpool = ctx.enter_context(tc.tile_pool(name="xpool", bufs=XBUFS))
        zpool = ctx.enter_context(tc.tile_pool(name="zpool", bufs=12))
        small = ctx.enter_context(tc.tile_pool(name="small", bufs=4))
        plpool = ctx.enter_context(tc.tile_pool(name="plpool", bufs=3))
        gqpool = ctx.enter_context(tc.tile_pool(name="gqpool", bufs=2))
        xcpool = ctx.enter_context(tc.tile_pool(name="xcpool", bufs=3))
        ypool = ctx.enter_context(tc.tile_pool(name="ypool", bufs=3))
        wstage = ctx.enter_context(tc.tile_pool(name="wstage", bufs=2))
        pst = ctx.enter_context(tc.psum_pool(name="pst", bufs=6))
        psy = ctx.enter_context(tc.psum_pool(name="psy", bufs=2))
        ctx.enter_context(tc.manual_schedule())

        x_t = {}
        mv_t = {}
        std_t = {}
        rstd_t = {}
        negmu_t = {}
        nmr_t = {}
        z_t = {}
        pl_t = {}
        xc_t = {}
        xsc_t = {}
        wg_t = {}

        def live(u):
            return 0 <= u < UNITS

        def load_x(u):
            xt = xpool.tile([P, ROWT, K], BF16, tag="x", name="xt%d" % u)
            rows = xv[u * UNIT:(u + 1) * UNIT, :].rearrange("(j p) k -> p j k", p=P)
            if u == 0:
                for j in range(ROWT):
                    nc.sync.dma_start(out=xt[:, j, :], in_=rows[:, j, :])
            else:
                nc.sync.dma_start(out=xt[:], in_=rows)
            x_t[u] = xt

        w_raw = []
        for g in range(G):
            wr = const.tile([P, OT, K], BF16, name="wraw%d" % g)
            w_raw.append(wr)

        def load_w(g):
            nc.sync.dma_start(out=w_raw[g][:], in_=W[g].rearrange("(t o) k -> o t k", t=OT))

        load_x(0)
        prm = const.tile([P, P], BF16, name="prm")
        nc.vector.memset(prm[:], 0.0)
        eps_t = const.tile([P, 1], F32, name="eps_t")
        nc.vector.memset(eps_t[:], EPS)
        nc.sync.dma_start(out=prm[0:32, :], in_=ln_gamma.rearrange("g (c p) -> (g c) p", p=P))
        nc.sync.dma_start(out=prm[32:64, :], in_=ln_beta.rearrange("g (c p) -> (g c) p", p=P))
        nc.sync.dma_start(out=prm[64:72, :], in_=b.rearrange("g (c p) -> (g c) p", p=P))
        load_w(0)
        for u in range(1, XBUFS - 2):
            load_x(u)

        warm = const.tile([P, 1], F32, name="warm")
        nc.scalar.activation(out=warm[:], in_=eps_t[:], func=ACT.Sqrt)

        ident_b = const.tile([P, P], BF16, name="ident_b")
        make_identity(nc, ident_b[:])
        ident_f = const.tile([P, P], F32, name="ident_f")
        make_identity(nc, ident_f[:])

        prm_ps = pst.tile([P, P], BF16, tag="zt", name="prm_ps")
        nc.tensor.transpose(prm_ps[:], prm[:], ident_b[:])
        cols = const.tile([P, P], F32, name="cols")
        nc.scalar.copy(out=cols[:], in_=prm_ps[:])

        wc = const.tile([P, G, PASSES, O], U32, name="wc", align_bytes=64)
        ws = const.tile([P, G, PASSES, O], U8, name="ws", align_bytes=64)

        def w_transpose(g, c2):
            wt = pst.tile([P, OT, 4, P], BF16, tag="zt", name="wt%d_%d" % (g, c2))
            for a in range(OT):
                for t in range(4):
                    c = c2 * 4 + t
                    nc.tensor.transpose(wt[:, a, t, :], w_raw[g][:, a, c * P:(c + 1) * P], ident_b[:])
            wg = wstage.tile([P, OT, P, 4], BF16, tag="wg", name="wg%d_%d" % (g, c2), align_bytes=64)
            nc.scalar.copy(out=wg[:], in_=wt[:].rearrange("p a t o -> p a o t"))
            wg_t[(g, c2)] = wg

        def w_quantise(g, c2):
            nc.vector.quantize_mx(
                out=wc[:, g, c2, :].bitcast(FP8X4),
                scales=ws[:, g, c2, :],
                in_=wg_t[(g, c2)][:].rearrange("p a o t -> p (a o t)"),
            )

        w_when = {}
        for g in range(G):
            w_when[max(UPG * g - 2, -1)] = (g, 0)
            w_when[max(UPG * g - 1, 0)] = (g, 1)

        st_t = {}

        def bn(u, j, h):
            if u not in st_t:
                st_t[u] = small.tile([P, ROWT, 2, 6], F32, tag="st", name="st%d" % u)
                mv_t[u] = small.tile([P, ROWT, 2], F32, tag="mv", name="mv%d" % u)
            nc.vector.bn_stats(out=st_t[u][:, j, h, :], in_=x_t[u][:, j, h * 512:(h + 1) * 512])

        def aggr(u, j):
            nc.vector.bn_aggr(out=mv_t[u][:, j, :], in_=st_t[u][:, j, :, :].rearrange("p h s -> p (h s)"))

        def sqrt_(u):
            std = small.tile([P, ROWT], F32, tag="std", name="std%d" % u)
            nc.scalar.activation(out=std[:], in_=mv_t[u][:, :, 1], func=ACT.Sqrt, bias=eps_t[:], scale=1.0)
            std_t[u] = std

        def recip(u):
            rstd_t[u] = small.tile([P, ROWT], F32, tag="rstd", name="rstd%d" % u)
            nc.vector.reciprocal(out=rstd_t[u][:], in_=std_t[u][:])

        def negmean(u):
            negmu_t[u] = small.tile([P, ROWT], F32, tag="negmu", name="negmu%d" % u)
            nc.scalar.activation(out=negmu_t[u][:], in_=mv_t[u][:, :, 0], func=ACT.Copy, scale=-1.0)

        def negmean_rstd(u):
            nmr_t[u] = small.tile([P, ROWT], F32, tag="nmr", name="nmr%d" % u)
            for j in range(ROWT):
                if Z_ENGINE[j] == "s":
                    nc.scalar.activation(out=nmr_t[u][:, j:j + 1], in_=negmu_t[u][:, j:j + 1], func=ACT.Copy,
                                         scale=rstd_t[u][:, j:j + 1])

        def zrow(u, j, eng):
            z = zpool.tile([P, K], F32, tag="z", name="z%d_%d" % (u, j))
            xin = x_t[u][:, j, :]
            if eng == "g":
                nc.gpsimd.tensor_scalar(out=z[:], in0=xin, scalar1=negmu_t[u][:, j:j + 1],
                                        scalar2=rstd_t[u][:, j:j + 1], op0=ALU.add, op1=ALU.mult)
            elif eng == "v":
                nc.vector.tensor_scalar(out=z[:], in0=xin, scalar1=negmu_t[u][:, j:j + 1],
                                        scalar2=rstd_t[u][:, j:j + 1], op0=ALU.add, op1=ALU.mult)
            else:
                nc.scalar.activation(out=z[:], in_=xin, func=ACT.Identity,
                                     scale=rstd_t[u][:, j:j + 1], bias=nmr_t[u][:, j:j + 1])
            z_t[(u, j)] = z

        def bank(u, c):
            g = u // UPG
            zp = pst.tile([P, UNIT], F32, tag="zt", name="zp%d_%d" % (u, c))
            for j in range(ROWT):
                nc.tensor.transpose(zp[:, j * P:(j + 1) * P], z_t[(u, j)][:, c * P:(c + 1) * P], ident_f[:])
            gi = g * CHUNKS + c
            nc.scalar.activation(out=pl_t[u][:, c, :], in_=zp[:], func=ACT.Identity,
                                 scale=cols[:, gi:gi + 1], bias=cols[:, 32 + gi:33 + gi])

        gq_t = {}

        def regroup(u, c2, eng, n0, n1):
            if u not in gq_t:
                gq_t[u] = gqpool.tile([P, PASSES, UNIT, 4], BF16, tag="gq", name="gq%d" % u, align_bytes=64)
            dst = gq_t[u][:, c2, n0:n1, :].rearrange("p (c i) t -> p c t i", i=4)
            src = pl_t[u][:, c2 * 4:(c2 + 1) * 4, n0:n1].rearrange("p t (c i) -> p c t i", i=4)
            if eng == "v":
                nc.vector.tensor_copy(out=dst, in_=src)
            else:
                nc.scalar.copy(out=dst, in_=src)

        def quantise(u, c2):
            if u not in xc_t:
                xc_t[u] = xcpool.tile([P, PASSES, UNIT], U32, tag="xc", name="xc%d" % u, align_bytes=64)
                xsc_t[u] = xcpool.tile([P, PASSES, UNIT], U8, tag="xsc", name="xsc%d" % u, align_bytes=64)
            nc.vector.quantize_mx(
                out=xc_t[u][:, c2, :].bitcast(FP8X4),
                scales=xsc_t[u][:, c2, :],
                in_=gq_t[u][:, c2, :, :].rearrange("p n t -> p (n t)"),
            )

        def multiply_store(u):
            g = u // UPG
            q = u % UPG
            last = u == UNITS - 1
            ysb = ypool.tile([P, OT, UNIT], F32, tag="y", name="y%d" % u)
            yps = []
            for a in range(OT):
                yp = psy.tile([P, UNIT], F32, tag="yp", name="yp%d_%d" % (u, a))
                yps.append(yp)
            for c2 in range(PASSES):
                for a in range(OT):
                    nc.tensor.matmul_mx(
                        out=yps[a][:],
                        lhsT=wc[:, g, c2, a * P:(a + 1) * P].bitcast(FP8X4),
                        lhsT_scale=ws[:, g, c2, a * P:(a + 1) * P],
                        rhs=xc_t[u][:, c2, :].bitcast(FP8X4),
                        rhs_scale=xsc_t[u][:, c2, :],
                        start=(c2 == 0),
                        stop=(c2 == PASSES - 1),
                    )
            dst = ov[g * O:(g + 1) * O, q * UNIT:(q + 1) * UNIT].rearrange("(t o) n -> o t n", t=OT)
            for a in range(OT):
                bi = 64 + g * OT + a
                if last and a == 1:
                    nc.vector.tensor_scalar(out=ysb[:, a, :], in0=yps[a][:], scalar1=cols[:, bi:bi + 1],
                                            scalar2=None, op0=ALU.add)
                else:
                    nc.scalar.activation(out=ysb[:, a, :], in_=yps[a][:], func=ACT.Identity,
                                         bias=cols[:, bi:bi + 1], scale=1.0)
                if last:
                    nc.sync.dma_start(out=dst[:, a, :], in_=ysb[:, a, :])
            if not last:
                nc.sync.dma_start(out=dst, in_=ysb[:])

        for i in range(-1, UNITS + 2):
            if live(i + XBUFS - 1):
                load_x(i + XBUFS - 1)
            if i >= 0 and i % UPG == 0 and i // UPG + 1 < G:
                load_w(i // UPG + 1)
            if live(i):
                sqrt_(i)
                negmean(i)
            last_a = i - 2 == UNITS - 1
            if live(i - 2):
                regroup(i - 2, 0, "v", 0, UNIT)
                if not last_a:
                    regroup(i - 2, 1, "v", 0, UNIT - S_COLS)
                quantise(i - 2, 0)
            if (i - 1) in w_when:
                w_quantise(*w_when[i - 1])
            if last_a:
                regroup(i - 2, 1, "v", 0, UNIT)
            if live(i):
                recip(i)
            if live(i - 2):
                quantise(i - 2, 1)
            z_eng = Z_LAST if i == UNITS - 1 else Z_ENGINE
            if live(i):
                for j in range(ROWT):
                    if z_eng[j] != "s":
                        zrow(i, j, z_eng[j])
            if live(i - 1):
                pl_t[i - 1] = plpool.tile([P, CHUNKS, UNIT], BF16, tag="pl", name="pl%d" % (i - 1))
                for c in range(CHUNKS):
                    bank(i - 1, c)
                    if c == 5 and live(i) and "s" in z_eng:
                        negmean_rstd(i)
            elif live(i) and "s" in z_eng:
                negmean_rstd(i)
            if live(i):
                for j in range(ROWT):
                    if z_eng[j] == "s":
                        zrow(i, j, "s")
            if live(i - 1) and i - 1 != UNITS - 1:
                regroup(i - 1, 1, "s", UNIT - S_COLS, UNIT)
            if live(i - 2):
                multiply_store(i - 2)
            if i in w_when:
                w_transpose(*w_when[i])
            if live(i + 1):
                for j in range(ROWT):
                    bn(i + 1, j, 0)
                    bn(i + 1, j, 1)
                for j in range(ROWT):
                    aggr(i + 1, j)
